import numpy as np
import ml_dtypes


def mxq(x, axis, fmt="e4m3"):
    dtype, down = {"e4m3": (ml_dtypes.float8_e4m3fn, 7), "e5m2": (ml_dtypes.float8_e5m2, 14)}[fmt]
    v = np.moveaxis(np.asarray(x, np.float32).astype(ml_dtypes.bfloat16).astype(np.float64), axis, -1)
    blocks = v.reshape(v.shape[:-1] + (-1, 32))
    amax = np.abs(blocks).max(-1, keepdims=True)
    byte = np.maximum(np.where(amax > 0, np.frexp(amax)[1] - 1 + 127, 0) - down, 1)
    scale = np.exp2(byte - 127.0)
    codes = (blocks / scale).astype(np.float32).astype(dtype).astype(np.float64)
    return np.moveaxis((codes * scale).reshape(v.shape), -1, axis)


WIDE = False


def mx_kscale(k):
    if not WIDE:
        return np.ones(k)
    levels = np.array([10, -10, 5, -5, 0])
    if k % 512:
        return np.exp2(np.random.permutation(np.resize(levels, k // 32))).repeat(32)
    a = np.empty((k // 512, 16))
    for p in range(k // 512):
        a[p, :8] = np.random.permutation(np.resize(levels, 8))
        for g in range(8):
            far = levels[np.abs(levels - a[p, g]) >= 10]
            a[p, g + 8] = far[np.random.randint(len(far))]
    return np.exp2(a.ravel()).repeat(32)


BF16 = ml_dtypes.bfloat16


def bf(x):
    return np.asarray(x, np.float32).astype(BF16)


def f64(x):
    return np.asarray(x).astype(np.float64)


G, GI, GO, B = 32, 32, 32, 4096
K = G * GI
N = G * GO


def block_gain():
    gain = np.ones((N, K))
    for g in range(G):
        gain[g * GO:(g + 1) * GO, g * GI:(g + 1) * GI] = 0.5
    return gain


def setup_inputs():
    s = mx_kscale(K)
    bound = 1.0 / np.sqrt(K)
    W = np.random.uniform(-bound, bound, (N, K)) * block_gain()
    return {"data": bf(np.random.standard_normal((B, K)) * s),
            "W": bf(W / s[None, :]),
            "b": bf(np.random.standard_normal(N) * 0.3)}


def reference(data, W, b):
    return (mxq(f64(data), 1, "e4m3") @ mxq(f64(W), 1, "e4m3").T) + f64(b)

@@ -1,0 +1,243 @@
+from contextlib import ExitStack
+
+import concourse.mybir as mybir
+from concourse.masks import make_identity
+
+F32 = mybir.dt.float32
+BF16 = mybir.dt.bfloat16
+U32 = mybir.dt.uint32
+U8 = mybir.dt.uint8
+FP8X4 = mybir.dt.float8_e4m3fn_x4
+ADD = mybir.AluOpType.add
+
+P = 128
+B = 4096
+K = 1024
+N = 1024
+FLOPS = 2 * B * K * N
+NT = B // P
+KW = K // 2
+NB = 512
+QT = 256
+ST = 4
+BANKS = 8
+
+GROUPS = [1,1,2,4,4,4,4,4,4,2,2]
+LOADS = [("x", 0, 1), ("w", 0, 1), ("w", 1, 1), ("w", 2, 1), ("w", 3, 1), ("x", 1, 1), ("x", 2, 2),
+         ("w", 4, 1), ("w", 5, 1), ("w", 6, 1), ("w", 7, 1), ("x", 4, 4), ("x", 8, 4), ("x", 12, 4), ("x", 16, 8), ("x", 24, 8)]
+UNITS = [8,8,8,4,4,4,4,4,4,2,2,2,2,2,2,2,1,1]
+WARM = 0
+WARM_EACH = 0
+
+
+def tile_groupfc_kernel(tc, data, W, b, out):
+    nc = tc.nc
+    assert sum(GROUPS) == NT and sum(UNITS) == 2 * NT
+    with ExitStack() as ctx:
+        const = ctx.enter_context(tc.tile_pool(name="const", bufs=1))
+        grp = ctx.enter_context(tc.tile_pool(name="grp", bufs=3))
+        stage = ctx.enter_context(tc.tile_pool(name="stage", bufs=4))
+        psum = ctx.enter_context(tc.psum_pool(name="psum", bufs=1))
+        ctx.enter_context(tc.manual_schedule())
+
+        data_v = data.rearrange("(p t) k -> p (t k)", t=NT)
+        out_v = out.rearrange("(p t) n -> p (t n)", t=NT)
+        w_v = W.rearrange("(t p) k -> t p k", p=P)
+
+        b1 = const.tile([1, N], BF16, name="b1")
+        nc.scalar.dma_start(out=b1[:], in_=b.unsqueeze(0))
+        ones = const.tile([P, P], BF16, name="ones")
+        nc.vector.memset(ones[:], 1.0)
+        brow = const.tile([P, N], BF16, name="brow")
+        nc.vector.memset(brow[:], 0.0)
+        scr = const.tile([P, 8], F32, name="scr")
+        nc.scalar.copy(out=scr[:, 0:1], in_=ones[:, 0:1])
+        ident = const.tile([P, P], F32, name="ident")
+        make_identity(nc, ident[:])
+        bias = const.tile([P, N], F32, name="bias")
+
+        w_sb = {}
+        x_at = {}
+        for kind, t0, n in LOADS:
+            if kind == "w":
+                wt = const.tile([P, K], BF16, name="w%d" % t0)
+                nc.sync.dma_start(out=wt[:], in_=w_v[t0])
+                w_sb[t0] = wt
+            else:
+                xt = const.tile([P, n * K], BF16, name="x%d" % t0)
+                nc.sync.dma_start(out=xt[:], in_=data_v[:, t0 * K:(t0 + n) * K])
+                for i in range(n):
+                    x_at[t0 + i] = (xt[:].bitcast(F32), i * KW)
+        nc.vector.tensor_copy(out=brow[0:1, :], in_=b1[:])
+
+        gw = []
+        gw_f = []
+        wq = []
+        ws = []
+        for h in range(2):
+            gwh = const.tile([P, 2 * NB * 4], BF16, name="gw%d" % h, align_bytes=64)
+            gw.append(gwh)
+            gw_f.append(gwh[:].bitcast(F32).rearrange("p (g n u) -> p g n u", g=2, u=2))
+            wq.append(const.tile([P, 2 * NB], U32, name="wq%d" % h, align_bytes=64))
+            ws.append(const.tile([P, 2 * NB], U8, name="ws%d" % h, align_bytes=64))
+
+        ring = [0]
+
+        def new_bank():
+            i = ring[0] % BANKS
+            ring[0] += 1
+            return psum.tile([P, NB], F32, name="ps%d" % i, tag="ps%d" % i)
+
+        def dummies(n):
+            if n > 0:
+                dm = new_bank()
+                for i in range(n):
+                    nc.tensor.matmul(out=dm[:], lhsT=ones[:], rhs=brow[:, NB:2 * NB], start=True, stop=True)
+
+        def transposes(src_f32, off):
+            pt = new_bank()
+            for g in range(2):
+                for u in range(2):
+                    c = 2 * g + u
+                    w0 = off + g * 2 * P
+                    nc.tensor.transpose(pt[:, c * P:(c + 1) * P], src_f32[:, w0 + u:w0 + 2 * P:2], ident[:])
+            return pt[:].rearrange("p (g u r) -> p g r u", g=2, u=2)
+
+        def tw(t):
+            h = t // 4
+            n0 = (t % 4) * P
+            src = transposes(w_sb[t][:].bitcast(F32), 0)
+            dst = gw_f[h][:, :, n0:n0 + P, :]
+            if t % 2 == 0:
+                nc.scalar.copy(out=dst, in_=src)
+            else:
+                nc.vector.tensor_copy(out=dst, in_=src)
+            dummies(WARM_EACH)
+
+        def qw(t):
+            h = t // 4
+            for g in range(2):
+                c0 = g * NB + (t % 4) * P
+                nc.vector.quantize_mx(
+                    out=wq[h][:, c0:c0 + P].bitcast(FP8X4),
+                    scales=ws[h][:, c0:c0 + P],
+                    in_=gw[h][:, 4 * c0:4 * (c0 + P)],
+                )
+
+        xg = {}
+        xq = {}
+        xs = {}
+        first = [sum(GROUPS[:j]) for j in range(len(GROUPS))]
+        HEAD = 3
+
+        def tr(j):
+            r = GROUPS[j]
+            if j < HEAD:
+                xg[j] = const.tile([P, r * K], BF16, name="xgh%d" % j, align_bytes=64)
+            else:
+                xg[j] = grp.tile([P, r * K], BF16, name="xg", tag="xg", align_bytes=64)
+            xg_f = xg[j][:].bitcast(F32)
+            for l in range(r):
+                src_f32, off = x_at[first[j] + l]
+                src = transposes(src_f32, off)
+                dst = xg_f[:, l * KW:(l + 1) * KW].rearrange("p (g r u) -> p g r u", g=2, u=2)
+                nc.scalar.copy(out=dst, in_=src)
+
+        def qx(j):
+            r = GROUPS[j]
+            if j < HEAD:
+                xq[j] = const.tile([P, r * QT], U32, name="xqh%d" % j, align_bytes=64)
+                xs[j] = const.tile([P, r * QT], U8, name="xsh%d" % j, align_bytes=64)
+            else:
+                xq[j] = grp.tile([P, r * QT], U32, name="xq", tag="xq", align_bytes=64)
+                xs[j] = grp.tile([P, r * QT], U8, name="xs", tag="xs", align_bytes=64)
+            nc.vector.quantize_mx(out=xq[j][:].bitcast(FP8X4), scales=xs[j][:], in_=xg[j][:])
+
+        unit_of = []
+        unit_b0 = []
+        left = []
+        for i in range(len(UNITS)):
+            unit_b0.append(len(unit_of))
+            left.append(UNITS[i])
+            for k in range(UNITS[i]):
+                unit_of.append(i)
+        staging = {}
+
+        def bank(j, l, h):
+            t = first[j] + l
+            bk = 2 * t + h
+            s = t // ST
+            if s not in staging:
+                staging[s] = stage.tile([P, ST * N], F32, name="ot", tag="ot")
+            ot = staging[s]
+            acc = new_bank()
+            for g in range(2):
+                a0 = l * QT + g * P
+                nc.tensor.matmul_mx(
+                    out=acc[:],
+                    lhsT=xq[j][:, a0:a0 + P].bitcast(FP8X4),
+                    lhsT_scale=xs[j][:, a0:a0 + P],
+                    rhs=wq[h][:, g * NB:(g + 1) * NB].bitcast(FP8X4),
+                    rhs_scale=ws[h][:, g * NB:(g + 1) * NB],
+                    start=(g == 0),
+                    stop=(g == 1),
+                )
+            o0 = (bk % (2 * ST)) * NB
+            nc.vector.tensor_tensor(out=ot[:, o0:o0 + NB], in0=acc[:], in1=bias[:, h * NB:(h + 1) * NB], op=ADD)
+            i = unit_of[bk]
+            left[i] -= 1
+            if left[i] == 0:
+                b0 = unit_b0[i]
+                c0 = (b0 % (2 * ST)) * NB
+                w = UNITS[i] * NB
+                nc.sync.dma_start(out=out_v[:, b0 * NB:b0 * NB + w], in_=ot[:, c0:c0 + w])
+
+        def mm(j, hs):
+            for l in range(GROUPS[j]):
+                for h in hs:
+                    bank(j, l, h)
+
+        dummies(WARM)
+        tr(0)
+        tw(0)
+        tw(1)
+        qx(0)
+        qw(0)
+        tw(2)
+        qw(1)
+        tw(3)
+        qw(2)
+        tr(1)
+        for h in range(2):
+            pb = new_bank()
+            nc.tensor.matmul(out=pb[:], lhsT=ones[:], rhs=brow[:, h * NB:(h + 1) * NB], start=True, stop=True)
+            nc.scalar.copy(out=bias[:, h * NB:(h + 1) * NB], in_=pb[:])
+        qw(3)
+        tr(2)
+        qx(1)
+        tw(4)
+        tw(5)
+        qx(2)
+        qw(4)
+        tw(6)
+        qw(5)
+        tw(7)
+        qw(6)
+        qw(7)
+        mm(0, [0])
+        mm(1, [0])
+        mm(2, [0])
+        tr(3)
+        mm(0, [1])
+        mm(1, [1])
+        tr(4)
+        qx(3)
+        mm(2, [1])
+        qx(4)
+        ng = len(GROUPS)
+        for j in range(HEAD, ng):
+            if j + 2 < ng:
+                tr(j + 2)
+            mm(j, [0, 1])
+            if j + 2 < ng:
+                qx(j + 2)

@@ -22,12 +22,14 @@ QT = 256
 ST = 4
 BANKS = 8
 
-GROUPS = [1,1,2,4,4,4,4,4,4,2,2]
-LOADS = [("x", 0, 1), ("w", 0, 1), ("w", 1, 1), ("w", 2, 1), ("w", 3, 1), ("x", 1, 1), ("x", 2, 2),
-         ("w", 4, 1), ("w", 5, 1), ("w", 6, 1), ("w", 7, 1), ("x", 4, 4), ("x", 8, 4), ("x", 12, 4), ("x", 16, 8), ("x", 24, 8)]
-UNITS = [8,8,8,4,4,4,4,4,4,2,2,2,2,2,2,2,1,1]
-WARM = 0
-WARM_EACH = 0
+GROUPS = [1, 1, 2, 2, 2, 4, 4, 4, 4, 4, 2, 2]
+LOADS = [("w", 0, 1), ("w", 1, 1), ("w", 2, 1), ("w", 3, 1), ("x", 0, 1), ("x", 1, 1), ("x", 2, 2),
+         ("x", 4, 2), ("w", 4, 1), ("w", 5, 1), ("x", 6, 2), ("w", 6, 1), ("w", 7, 1),
+         ("x", 8, 4), ("x", 12, 4), ("x", 16, 4), ("x", 20, 4), ("x", 24, 4)]
+UNITS = [8, 8, 8, 4, 4, 4, 4, 4, 4, 2, 2, 2, 2, 2, 2, 2, 1, 1]
+HEAD_TILES = 8
+WARM = 5
+KEEP = 1
 
 
 def tile_groupfc_kernel(tc, data, W, b, out):
@@ -35,7 +37,10 @@ def tile_groupfc_kernel(tc, data, W, b, out):
     assert sum(GROUPS) == NT and sum(UNITS) == 2 * NT
     with ExitStack() as ctx:
         const = ctx.enter_context(tc.tile_pool(name="const", bufs=1))
-        grp = ctx.enter_context(tc.tile_pool(name="grp", bufs=3))
+        xin = ctx.enter_context(tc.tile_pool(name="xin", bufs=5))
+        grp = ctx.enter_context(tc.tile_pool(name="grp", bufs=2))
+        gath = ctx.enter_context(tc.tile_pool(name="gath", bufs=2))
+        prep = ctx.enter_context(tc.tile_pool(name="prep", bufs=5))
         stage = ctx.enter_context(tc.tile_pool(name="stage", bufs=4))
         psum = ctx.enter_context(tc.psum_pool(name="psum", bufs=1))
         ctx.enter_context(tc.manual_schedule())
@@ -58,17 +63,23 @@ def tile_groupfc_kernel(tc, data, W, b, out):
 
         w_sb = {}
         x_at = {}
-        for kind, t0, n in LOADS:
+
+        def load(kind, t0, n):
             if kind == "w":
                 wt = const.tile([P, K], BF16, name="w%d" % t0)
                 nc.sync.dma_start(out=wt[:], in_=w_v[t0])
                 w_sb[t0] = wt
             else:
-                xt = const.tile([P, n * K], BF16, name="x%d" % t0)
+                if n < 4:
+                    xt = const.tile([P, n * K], BF16, name="x%d" % t0)
+                else:
+                    xt = xin.tile([P, n * K], BF16, name="xin", tag="xin")
                 nc.sync.dma_start(out=xt[:], in_=data_v[:, t0 * K:(t0 + n) * K])
                 for i in range(n):
                     x_at[t0 + i] = (xt[:].bitcast(F32), i * KW)
-        nc.vector.tensor_copy(out=brow[0:1, :], in_=b1[:])
+
+        for kind, t0, n in LOADS:
+            load(kind, t0, n)
 
         gw = []
         gw_f = []
@@ -91,28 +102,61 @@ def tile_groupfc_kernel(tc, data, W, b, out):
         def dummies(n):
             if n > 0:
                 dm = new_bank()
+                ring[0] -= 1
                 for i in range(n):
                     nc.tensor.matmul(out=dm[:], lhsT=ones[:], rhs=brow[:, NB:2 * NB], start=True, stop=True)
 
-        def transposes(src_f32, off):
+        def copy_on(eng, out, in_):
+            if eng == "s":
+                nc.scalar.copy(out=out, in_=in_)
+            else:
+                nc.vector.tensor_copy(out=out, in_=in_)
+
+        def transposes(words, off):
             pt = new_bank()
             for g in range(2):
                 for u in range(2):
                     c = 2 * g + u
                     w0 = off + g * 2 * P
-                    nc.tensor.transpose(pt[:, c * P:(c + 1) * P], src_f32[:, w0 + u:w0 + 2 * P:2], ident[:])
+                    nc.tensor.transpose(pt[:, c * P:(c + 1) * P], words[:, w0 + u:w0 + 2 * P:2], ident[:])
             return pt[:].rearrange("p (g u r) -> p g r u", g=2, u=2)
 
-        def tw(t):
+        def transposes_ordered(words):
+            pt = new_bank()
+            for g in range(2):
+                for u in range(2):
+                    c = 2 * g + u
+                    w0 = u * 2 * P + g * P
+                    nc.tensor.transpose(pt[:, c * P:(c + 1) * P], words[:, w0:w0 + P], ident[:])
+            return pt[:].rearrange("p (g u r) -> p g r u", g=2, u=2)
+
+        xp = {}
+
+        def order(eng, words, off, key):
+            pt = prep.tile([P, KW], F32, name="xp", tag="xp")
+            copy_on(
+                eng,
+                pt[:].rearrange("p (u w) -> p u w", u=2),
+                words[:, off:off + KW].rearrange("p (w u) -> p u w", u=2),
+            )
+            xp[key] = pt
+
+        def pre(eng, *tiles):
+            for t in tiles:
+                words, off = x_at[t]
+                order(eng, words, off, t)
+
+        def prew(eng, t):
+            order(eng, w_sb[t][:].bitcast(F32), 0, ("w", t))
+
+        def tw(eng, t):
             h = t // 4
             n0 = (t % 4) * P
-            src = transposes(w_sb[t][:].bitcast(F32), 0)
-            dst = gw_f[h][:, :, n0:n0 + P, :]
-            if t % 2 == 0:
-                nc.scalar.copy(out=dst, in_=src)
+            if ("w", t) in xp:
+                src = transposes_ordered(xp[("w", t)])
             else:
-                nc.vector.tensor_copy(out=dst, in_=src)
-            dummies(WARM_EACH)
+                src = transposes(w_sb[t][:].bitcast(F32), 0)
+            copy_on(eng, gw_f[h][:, :, n0:n0 + P, :], src)
 
         def qw(t):
             h = t // 4
@@ -124,28 +168,44 @@ def tile_groupfc_kernel(tc, data, W, b, out):
                     in_=gw[h][:, 4 * c0:4 * (c0 + P)],
                 )
 
+        bias_ps = {}
+
+        def bias_mm(h):
+            bias_ps[h] = new_bank()
+            nc.tensor.matmul(out=bias_ps[h][:], lhsT=ones[:], rhs=brow[:, h * NB:(h + 1) * NB], start=True, stop=True)
+
+        def bias_copy(eng, h):
+            copy_on(eng, bias[:, h * NB:(h + 1) * NB], bias_ps[h][:])
+
+        first = [sum(GROUPS[:j]) for j in range(len(GROUPS))]
+        group_of = {}
+        for j in range(len(GROUPS)):
+            for l in range(GROUPS[j]):
+                group_of[first[j] + l] = (j, l)
         xg = {}
         xq = {}
         xs = {}
-        first = [sum(GROUPS[:j]) for j in range(len(GROUPS))]
-        HEAD = 3
 
-        def tr(j):
-            r = GROUPS[j]
-            if j < HEAD:
-                xg[j] = const.tile([P, r * K], BF16, name="xgh%d" % j, align_bytes=64)
-            else:
-                xg[j] = grp.tile([P, r * K], BF16, name="xg", tag="xg", align_bytes=64)
-            xg_f = xg[j][:].bitcast(F32)
-            for l in range(r):
-                src_f32, off = x_at[first[j] + l]
-                src = transposes(src_f32, off)
-                dst = xg_f[:, l * KW:(l + 1) * KW].rearrange("p (g r u) -> p g r u", g=2, u=2)
-                nc.scalar.copy(out=dst, in_=src)
+        def tr(eng, *tiles):
+            for t in tiles:
+                j, l = group_of[t]
+                r = GROUPS[j]
+                if j not in xg:
+                    if t < HEAD_TILES:
+                        xg[j] = const.tile([P, r * K], BF16, name="xgh%d" % j, align_bytes=64)
+                    else:
+                        xg[j] = gath.tile([P, r * K], BF16, name="xg", tag="xg", align_bytes=64)
+                if t in xp:
+                    src = transposes_ordered(xp[t])
+                else:
+                    words, off = x_at[t]
+                    src = transposes(words, off)
+                dst = xg[j][:].bitcast(F32)[:, l * KW:(l + 1) * KW].rearrange("p (g r u) -> p g r u", g=2, u=2)
+                copy_on(eng, dst, src)
 
         def qx(j):
             r = GROUPS[j]
-            if j < HEAD:
+            if first[j] < HEAD_TILES:
                 xq[j] = const.tile([P, r * QT], U32, name="xqh%d" % j, align_bytes=64)
                 xs[j] = const.tile([P, r * QT], U8, name="xsh%d" % j, align_bytes=64)
             else:
@@ -163,8 +223,8 @@ def tile_groupfc_kernel(tc, data, W, b, out):
                 unit_of.append(i)
         staging = {}
 
-        def bank(j, l, h):
-            t = first[j] + l
+        def bank(t, h):
+            j, l = group_of[t]
             bk = 2 * t + h
             s = t // ST
             if s not in staging:
@@ -192,52 +252,73 @@ def tile_groupfc_kernel(tc, data, W, b, out):
                 w = UNITS[i] * NB
                 nc.sync.dma_start(out=out_v[:, b0 * NB:b0 * NB + w], in_=ot[:, c0:c0 + w])
 
-        def mm(j, hs):
-            for l in range(GROUPS[j]):
+        def mm(tiles, hs):
+            for t in tiles:
                 for h in hs:
-                    bank(j, l, h)
+                    bank(t, h)
 
         dummies(WARM)
-        tr(0)
-        tw(0)
-        tw(1)
-        qx(0)
+        nc.vector.tensor_copy(out=brow[0:1, :], in_=b1[:])
+        tw("s", 0)
+        tw("v", 1)
+        bias_mm(0)
+        bias_copy("s", 0)
+        dummies(KEEP)
+        tw("s", 2)
         qw(0)
-        tw(2)
+        tw("s", 3)
         qw(1)
-        tw(3)
+        dummies(KEEP)
+        tr("s", 0)
         qw(2)
-        tr(1)
-        for h in range(2):
-            pb = new_bank()
-            nc.tensor.matmul(out=pb[:], lhsT=ones[:], rhs=brow[:, h * NB:(h + 1) * NB], start=True, stop=True)
-            nc.scalar.copy(out=bias[:, h * NB:(h + 1) * NB], in_=pb[:])
+        dummies(KEEP)
+        tr("s", 1)
         qw(3)
-        tr(2)
+        qx(0)
         qx(1)
-        tw(4)
-        tw(5)
+        dummies(KEEP)
+        tr("s", 2, 3)
+        mm([0], [0])
         qx(2)
-        qw(4)
-        tw(6)
-        qw(5)
-        tw(7)
-        qw(6)
-        qw(7)
-        mm(0, [0])
-        mm(1, [0])
-        mm(2, [0])
-        tr(3)
-        mm(0, [1])
-        mm(1, [1])
-        tr(4)
+        mm([1], [0])
+        tr("s", 4, 5)
+        tw("s", 4)
+        pre("s", 8)
+        mm([2], [0])
         qx(3)
-        mm(2, [1])
+        mm([3], [0])
+        bias_mm(1)
+        bias_copy("s", 1)
+        tw("s", 5)
+        tr("s", 6, 7)
+        pre("s", 9)
+        qw(4)
+        mm([4], [0])
         qx(4)
+        mm([5], [0])
+        qw(5)
+        tw("s", 6)
+        tw("s", 7)
+        pre("s", 10, 11)
+        mm([6], [0])
+        qw(6)
+        mm([7], [0])
+        qw(7)
+        tr("s", 8, 9, 10, 11)
+        load("x", 28, 4)
+        pre("s", 12, 13, 14, 15)
+        mm([0, 1, 2, 3], [1])
+        qx(5)
+        mm([4, 5, 6, 7], [1])
+
         ng = len(GROUPS)
-        for j in range(HEAD, ng):
+        for j in range(5, ng):
+            if j + 1 < ng:
+                tr("s", *range(first[j + 1], first[j + 1] + GROUPS[j + 1]))
             if j + 2 < ng:
-                tr(j + 2)
-            mm(j, [0, 1])
-            if j + 2 < ng:
-                qx(j + 2)
+                pre("s", *range(first[j + 2], first[j + 2] + GROUPS[j + 2]))
+            half = GROUPS[j] // 2
+            mm(range(first[j], first[j] + half), [0, 1])
+            if j + 1 < ng:
+                qx(j + 1)
+            mm(range(first[j] + half, first[j] + GROUPS[j]), [0, 1])

@@ -28,7 +28,7 @@ LOADS = [("w", 0, 1), ("w", 1, 1), ("w", 2, 1), ("w", 3, 1), ("x", 0, 1), ("x", 
          ("x", 8, 4), ("x", 12, 4), ("x", 16, 4), ("x", 20, 4), ("x", 24, 4)]
 UNITS = [8, 8, 8, 4, 4, 4, 4, 4, 4, 2, 2, 2, 2, 2, 2, 2, 1, 1]
 HEAD_TILES = 8
-WARM = 5
+WARM = 3
 KEEP = 1
 
 
@@ -53,12 +53,14 @@ def tile_groupfc_kernel(tc, data, W, b, out):
         nc.scalar.dma_start(out=b1[:], in_=b.unsqueeze(0))
         ones = const.tile([P, P], BF16, name="ones")
         nc.vector.memset(ones[:], 1.0)
-        brow = const.tile([P, N], BF16, name="brow")
-        nc.vector.memset(brow[:], 0.0)
+        zero = const.tile([P, NB], BF16, name="zero")
+        nc.vector.memset(zero[:].bitcast(F32), 0.0)
         scr = const.tile([P, 8], F32, name="scr")
         nc.scalar.copy(out=scr[:, 0:1], in_=ones[:, 0:1])
         ident = const.tile([P, P], F32, name="ident")
         make_identity(nc, ident[:])
+        brow = const.tile([P, N], BF16, name="brow")
+        nc.gpsimd.memset(brow[:].bitcast(F32), 0.0)
         bias = const.tile([P, N], F32, name="bias")
 
         w_sb = {}
@@ -82,13 +84,11 @@ def tile_groupfc_kernel(tc, data, W, b, out):
             load(kind, t0, n)
 
         gw = []
-        gw_f = []
+        for t in range(8):
+            gw.append(const.tile([P, K], BF16, name="gw%d" % t, align_bytes=64))
         wq = []
         ws = []
         for h in range(2):
-            gwh = const.tile([P, 2 * NB * 4], BF16, name="gw%d" % h, align_bytes=64)
-            gw.append(gwh)
-            gw_f.append(gwh[:].bitcast(F32).rearrange("p (g n u) -> p g n u", g=2, u=2))
             wq.append(const.tile([P, 2 * NB], U32, name="wq%d" % h, align_bytes=64))
             ws.append(const.tile([P, 2 * NB], U8, name="ws%d" % h, align_bytes=64))
 
@@ -104,7 +104,7 @@ def tile_groupfc_kernel(tc, data, W, b, out):
                 dm = new_bank()
                 ring[0] -= 1
                 for i in range(n):
-                    nc.tensor.matmul(out=dm[:], lhsT=ones[:], rhs=brow[:, NB:2 * NB], start=True, stop=True)
+                    nc.tensor.matmul(out=dm[:], lhsT=ones[:], rhs=zero[:], start=True, stop=True)
 
         def copy_on(eng, out, in_):
             if eng == "s":
@@ -150,13 +150,11 @@ def tile_groupfc_kernel(tc, data, W, b, out):
             order(eng, w_sb[t][:].bitcast(F32), 0, ("w", t))
 
         def tw(eng, t):
-            h = t // 4
-            n0 = (t % 4) * P
             if ("w", t) in xp:
                 src = transposes_ordered(xp[("w", t)])
             else:
                 src = transposes(w_sb[t][:].bitcast(F32), 0)
-            copy_on(eng, gw_f[h][:, :, n0:n0 + P, :], src)
+            copy_on(eng, gw[t][:].bitcast(F32).rearrange("p (g r u) -> p g r u", g=2, u=2), src)
 
         def qw(t):
             h = t // 4
@@ -165,7 +163,7 @@ def tile_groupfc_kernel(tc, data, W, b, out):
                 nc.vector.quantize_mx(
                     out=wq[h][:, c0:c0 + P].bitcast(FP8X4),
                     scales=ws[h][:, c0:c0 + P],
-                    in_=gw[h][:, 4 * c0:4 * (c0 + P)],
+                    in_=gw[t][:, g * 4 * P:(g + 1) * 4 * P],
                 )
 
         bias_ps = {}
@@ -283,7 +281,6 @@ def tile_groupfc_kernel(tc, data, W, b, out):
         mm([1], [0])
         tr("s", 4, 5)
         tw("s", 4)
-        pre("s", 8)
         mm([2], [0])
         qx(3)
         mm([3], [0])
@@ -291,8 +288,8 @@ def tile_groupfc_kernel(tc, data, W, b, out):
         bias_copy("s", 1)
         tw("s", 5)
         tr("s", 6, 7)
-        pre("s", 9)
         qw(4)
+        pre("v", 8, 9)
         mm([4], [0])
         qx(4)
         mm([5], [0])

@@ -29,7 +29,7 @@ LOADS = [("w", 0, 1), ("w", 1, 1), ("w", 2, 1), ("w", 3, 1), ("x", 0, 1), ("x", 
 UNITS = [8, 8, 8, 4, 4, 4, 4, 4, 4, 2, 2, 2, 2, 2, 2, 2, 1, 1]
 HEAD_TILES = 8
 WARM = 3
-KEEP = 1
+KEEP = 0
 
 
 def tile_groupfc_kernel(tc, data, W, b, out):

from contextlib import ExitStack

import concourse.mybir as mybir
from concourse.masks import make_identity

F32 = mybir.dt.float32
BF16 = mybir.dt.bfloat16
U32 = mybir.dt.uint32
U8 = mybir.dt.uint8
FP8X4 = mybir.dt.float8_e4m3fn_x4
ADD = mybir.AluOpType.add

P = 128
B = 4096
K = 1024
N = 1024
FLOPS = 2 * B * K * N
NT = B // P
KW = K // 2
NB = 512
QT = 256
ST = 4
BANKS = 8

GROUPS = [1, 1, 2, 2, 2, 4, 4, 4, 4, 4, 2, 2]
LOADS = [("w", 0, 1), ("w", 1, 1), ("w", 2, 1), ("w", 3, 1), ("x", 0, 1), ("x", 1, 1), ("x", 2, 2),
         ("x", 4, 2), ("w", 4, 1), ("w", 5, 1), ("x", 6, 2), ("w", 6, 1), ("w", 7, 1),
         ("x", 8, 4), ("x", 12, 4), ("x", 16, 4), ("x", 20, 4), ("x", 24, 4)]
UNITS = [8, 8, 8, 4, 4, 4, 4, 4, 4, 2, 2, 2, 2, 2, 2, 2, 1, 1]
HEAD_TILES = 8
WARM = 3
KEEP = 0


def tile_groupfc_kernel(tc, data, W, b, out):
    nc = tc.nc
    assert sum(GROUPS) == NT and sum(UNITS) == 2 * NT
    with ExitStack() as ctx:
        const = ctx.enter_context(tc.tile_pool(name="const", bufs=1))
        xin = ctx.enter_context(tc.tile_pool(name="xin", bufs=5))
        grp = ctx.enter_context(tc.tile_pool(name="grp", bufs=2))
        gath = ctx.enter_context(tc.tile_pool(name="gath", bufs=2))
        prep = ctx.enter_context(tc.tile_pool(name="prep", bufs=5))
        stage = ctx.enter_context(tc.tile_pool(name="stage", bufs=4))
        psum = ctx.enter_context(tc.psum_pool(name="psum", bufs=1))
        ctx.enter_context(tc.manual_schedule())

        data_v = data.rearrange("(p t) k -> p (t k)", t=NT)
        out_v = out.rearrange("(p t) n -> p (t n)", t=NT)
        w_v = W.rearrange("(t p) k -> t p k", p=P)

        b1 = const.tile([1, N], BF16, name="b1")
        nc.scalar.dma_start(out=b1[:], in_=b.unsqueeze(0))
        ones = const.tile([P, P], BF16, name="ones")
        nc.vector.memset(ones[:], 1.0)
        zero = const.tile([P, NB], BF16, name="zero")
        nc.vector.memset(zero[:].bitcast(F32), 0.0)
        scr = const.tile([P, 8], F32, name="scr")
        nc.scalar.copy(out=scr[:, 0:1], in_=ones[:, 0:1])
        ident = const.tile([P, P], F32, name="ident")
        make_identity(nc, ident[:])
        brow = const.tile([P, N], BF16, name="brow")
        nc.gpsimd.memset(brow[:].bitcast(F32), 0.0)
        bias = const.tile([P, N], F32, name="bias")

        w_sb = {}
        x_at = {}

        def load(kind, t0, n):
            if kind == "w":
                wt = const.tile([P, K], BF16, name="w%d" % t0)
                nc.sync.dma_start(out=wt[:], in_=w_v[t0])
                w_sb[t0] = wt
            else:
                if n < 4:
                    xt = const.tile([P, n * K], BF16, name="x%d" % t0)
                else:
                    xt = xin.tile([P, n * K], BF16, name="xin", tag="xin")
                nc.sync.dma_start(out=xt[:], in_=data_v[:, t0 * K:(t0 + n) * K])
                for i in range(n):
                    x_at[t0 + i] = (xt[:].bitcast(F32), i * KW)

        for kind, t0, n in LOADS:
            load(kind, t0, n)

        gw = []
        for t in range(8):
            gw.append(const.tile([P, K], BF16, name="gw%d" % t, align_bytes=64))
        wq = []
        ws = []
        for h in range(2):
            wq.append(const.tile([P, 2 * NB], U32, name="wq%d" % h, align_bytes=64))
            ws.append(const.tile([P, 2 * NB], U8, name="ws%d" % h, align_bytes=64))

        ring = [0]

        def new_bank():
            i = ring[0] % BANKS
            ring[0] += 1
            return psum.tile([P, NB], F32, name="ps%d" % i, tag="ps%d" % i)

        def dummies(n):
            if n > 0:
                dm = new_bank()
                ring[0] -= 1
                for i in range(n):
                    nc.tensor.matmul(out=dm[:], lhsT=ones[:], rhs=zero[:], start=True, stop=True)

        def copy_on(eng, out, in_):
            if eng == "s":
                nc.scalar.copy(out=out, in_=in_)
            else:
                nc.vector.tensor_copy(out=out, in_=in_)

        def transposes(words, off):
            pt = new_bank()
            for g in range(2):
                for u in range(2):
                    c = 2 * g + u
                    w0 = off + g * 2 * P
                    nc.tensor.transpose(pt[:, c * P:(c + 1) * P], words[:, w0 + u:w0 + 2 * P:2], ident[:])
            return pt[:].rearrange("p (g u r) -> p g r u", g=2, u=2)

        def transposes_ordered(words):
            pt = new_bank()
            for g in range(2):
                for u in range(2):
                    c = 2 * g + u
                    w0 = u * 2 * P + g * P
                    nc.tensor.transpose(pt[:, c * P:(c + 1) * P], words[:, w0:w0 + P], ident[:])
            return pt[:].rearrange("p (g u r) -> p g r u", g=2, u=2)

        xp = {}

        def order(eng, words, off, key):
            pt = prep.tile([P, KW], F32, name="xp", tag="xp")
            copy_on(
                eng,
                pt[:].rearrange("p (u w) -> p u w", u=2),
                words[:, off:off + KW].rearrange("p (w u) -> p u w", u=2),
            )
            xp[key] = pt

        def pre(eng, *tiles):
            for t in tiles:
                words, off = x_at[t]
                order(eng, words, off, t)

        def prew(eng, t):
            order(eng, w_sb[t][:].bitcast(F32), 0, ("w", t))

        def tw(eng, t):
            if ("w", t) in xp:
                src = transposes_ordered(xp[("w", t)])
            else:
                src = transposes(w_sb[t][:].bitcast(F32), 0)
            copy_on(eng, gw[t][:].bitcast(F32).rearrange("p (g r u) -> p g r u", g=2, u=2), src)

        def qw(t):
            h = t // 4
            for g in range(2):
                c0 = g * NB + (t % 4) * P
                nc.vector.quantize_mx(
                    out=wq[h][:, c0:c0 + P].bitcast(FP8X4),
                    scales=ws[h][:, c0:c0 + P],
                    in_=gw[t][:, g * 4 * P:(g + 1) * 4 * P],
                )

        bias_ps = {}

        def bias_mm(h):
            bias_ps[h] = new_bank()
            nc.tensor.matmul(out=bias_ps[h][:], lhsT=ones[:], rhs=brow[:, h * NB:(h + 1) * NB], start=True, stop=True)

        def bias_copy(eng, h):
            copy_on(eng, bias[:, h * NB:(h + 1) * NB], bias_ps[h][:])

        first = [sum(GROUPS[:j]) for j in range(len(GROUPS))]
        group_of = {}
        for j in range(len(GROUPS)):
            for l in range(GROUPS[j]):
                group_of[first[j] + l] = (j, l)
        xg = {}
        xq = {}
        xs = {}

        def tr(eng, *tiles):
            for t in tiles:
                j, l = group_of[t]
                r = GROUPS[j]
                if j not in xg:
                    if t < HEAD_TILES:
                        xg[j] = const.tile([P, r * K], BF16, name="xgh%d" % j, align_bytes=64)
                    else:
                        xg[j] = gath.tile([P, r * K], BF16, name="xg", tag="xg", align_bytes=64)
                if t in xp:
                    src = transposes_ordered(xp[t])
                else:
                    words, off = x_at[t]
                    src = transposes(words, off)
                dst = xg[j][:].bitcast(F32)[:, l * KW:(l + 1) * KW].rearrange("p (g r u) -> p g r u", g=2, u=2)
                copy_on(eng, dst, src)

        def qx(j):
            r = GROUPS[j]
            if first[j] < HEAD_TILES:
                xq[j] = const.tile([P, r * QT], U32, name="xqh%d" % j, align_bytes=64)
                xs[j] = const.tile([P, r * QT], U8, name="xsh%d" % j, align_bytes=64)
            else:
                xq[j] = grp.tile([P, r * QT], U32, name="xq", tag="xq", align_bytes=64)
                xs[j] = grp.tile([P, r * QT], U8, name="xs", tag="xs", align_bytes=64)
            nc.vector.quantize_mx(out=xq[j][:].bitcast(FP8X4), scales=xs[j][:], in_=xg[j][:])

        unit_of = []
        unit_b0 = []
        left = []
        for i in range(len(UNITS)):
            unit_b0.append(len(unit_of))
            left.append(UNITS[i])
            for k in range(UNITS[i]):
                unit_of.append(i)
        staging = {}

        def bank(t, h):
            j, l = group_of[t]
            bk = 2 * t + h
            s = t // ST
            if s not in staging:
                staging[s] = stage.tile([P, ST * N], F32, name="ot", tag="ot")
            ot = staging[s]
            acc = new_bank()
            for g in range(2):
                a0 = l * QT + g * P
                nc.tensor.matmul_mx(
                    out=acc[:],
                    lhsT=xq[j][:, a0:a0 + P].bitcast(FP8X4),
                    lhsT_scale=xs[j][:, a0:a0 + P],
                    rhs=wq[h][:, g * NB:(g + 1) * NB].bitcast(FP8X4),
                    rhs_scale=ws[h][:, g * NB:(g + 1) * NB],
                    start=(g == 0),
                    stop=(g == 1),
                )
            o0 = (bk % (2 * ST)) * NB
            nc.vector.tensor_tensor(out=ot[:, o0:o0 + NB], in0=acc[:], in1=bias[:, h * NB:(h + 1) * NB], op=ADD)
            i = unit_of[bk]
            left[i] -= 1
            if left[i] == 0:
                b0 = unit_b0[i]
                c0 = (b0 % (2 * ST)) * NB
                w = UNITS[i] * NB
                nc.sync.dma_start(out=out_v[:, b0 * NB:b0 * NB + w], in_=ot[:, c0:c0 + w])

        def mm(tiles, hs):
            for t in tiles:
                for h in hs:
                    bank(t, h)

        dummies(WARM)
        nc.vector.tensor_copy(out=brow[0:1, :], in_=b1[:])
        tw("s", 0)
        tw("v", 1)
        bias_mm(0)
        bias_copy("s", 0)
        dummies(KEEP)
        tw("s", 2)
        qw(0)
        tw("s", 3)
        qw(1)
        dummies(KEEP)
        tr("s", 0)
        qw(2)
        dummies(KEEP)
        tr("s", 1)
        qw(3)
        qx(0)
        qx(1)
        dummies(KEEP)
        tr("s", 2, 3)
        mm([0], [0])
        qx(2)
        mm([1], [0])
        tr("s", 4, 5)
        tw("s", 4)
        mm([2], [0])
        qx(3)
        mm([3], [0])
        bias_mm(1)
        bias_copy("s", 1)
        tw("s", 5)
        tr("s", 6, 7)
        qw(4)
        pre("v", 8, 9)
        mm([4], [0])
        qx(4)
        mm([5], [0])
        qw(5)
        tw("s", 6)
        tw("s", 7)
        pre("s", 10, 11)
        mm([6], [0])
        qw(6)
        mm([7], [0])
        qw(7)
        tr("s", 8, 9, 10, 11)
        load("x", 28, 4)
        pre("s", 12, 13, 14, 15)
        mm([0, 1, 2, 3], [1])
        qx(5)
        mm([4, 5, 6, 7], [1])

        ng = len(GROUPS)
        for j in range(5, ng):
            if j + 1 < ng:
                tr("s", *range(first[j + 1], first[j + 1] + GROUPS[j + 1]))
            if j + 2 < ng:
                pre("s", *range(first[j + 2], first[j + 2] + GROUPS[j + 2]))
            half = GROUPS[j] // 2
            mm(range(first[j], first[j] + half), [0, 1])
            if j + 1 < ng:
                qx(j + 1)
            mm(range(first[j] + half, first[j] + GROUPS[j]), [0, 1])
